import numpy as np
import ml_dtypes


def mxq(x, axis, fmt="e4m3"):
    dtype, down = {"e4m3": (ml_dtypes.float8_e4m3fn, 7), "e5m2": (ml_dtypes.float8_e5m2, 14)}[fmt]
    v = np.moveaxis(np.asarray(x, np.float32).astype(ml_dtypes.bfloat16).astype(np.float64), axis, -1)
    blocks = v.reshape(v.shape[:-1] + (-1, 32))
    amax = np.abs(blocks).max(-1, keepdims=True)
    byte = np.maximum(np.where(amax > 0, np.frexp(amax)[1] - 1 + 127, 0) - down, 1)
    scale = np.exp2(byte - 127.0)
    codes = (blocks / scale).astype(np.float32).astype(dtype).astype(np.float64)
    return np.moveaxis((codes * scale).reshape(v.shape), -1, axis)


WIDE = False


def mx_kscale(k):
    if not WIDE:
        return np.ones(k)
    levels = np.array([10, -10, 5, -5, 0])
    if k % 512:
        return np.exp2(np.random.permutation(np.resize(levels, k // 32))).repeat(32)
    a = np.empty((k // 512, 16))
    for p in range(k // 512):
        a[p, :8] = np.random.permutation(np.resize(levels, 8))
        for g in range(8):
            far = levels[np.abs(levels - a[p, g]) >= 10]
            a[p, g + 8] = far[np.random.randint(len(far))]
    return np.exp2(a.ravel()).repeat(32)


BF16 = ml_dtypes.bfloat16


def bf(x):
    return np.asarray(x, np.float32).astype(BF16)


def f64(x):
    return np.asarray(x).astype(np.float64)


B, N, E, H, C = 1, 1024, 2048, 8, 512
D = E // H
EPS = 1e-5


def silu(t):
    return t / (1.0 + np.exp(-t))


def setup_inputs():
    t = mx_kscale(E)
    ret = np.random.standard_normal((B, N, H, D)) * 4.0 + np.random.standard_normal((B, N, H, 1)) * 2.0
    return {"ret": bf(ret.reshape(B, N, E)),
            "g": bf(np.random.standard_normal((B, N, E))),
            "gn_weight": bf((1.0 + 0.1 * np.random.standard_normal(E)) * t),
            "gn_bias": bf(0.1 * np.random.standard_normal(E) * t),
            "w_o": bf(np.random.standard_normal((E, E)) / np.sqrt(E) / t[:, None]),
            "b_o": bf(np.random.standard_normal(E) * 0.3)}


def reference(ret, g, gn_weight, gn_bias, w_o, b_o):
    r = f64(ret).reshape(B, N, H, D)
    mean = r.mean(axis=-1, keepdims=True)
    var = r.var(axis=-1, keepdims=True)
    r = (r - mean) / np.sqrt(var + EPS)
    rn = r.reshape(B, N, E) * f64(gn_weight) + f64(gn_bias)
    gate = silu(f64(g)) * rn
    return (mxq(gate, 2, "e4m3") @ mxq(f64(w_o), 0, "e4m3")) + f64(b_o)

@@ -1,0 +1,317 @@
+from contextlib import ExitStack
+
+import concourse.mybir as mybir
+from concourse.masks import make_identity
+
+F32 = mybir.dt.float32
+BF16 = mybir.dt.bfloat16
+U32 = mybir.dt.uint32
+U8 = mybir.dt.uint8
+FP8X4 = mybir.dt.float8_e4m3fn_x4
+ACT = mybir.ActivationFunctionType
+ALU = mybir.AluOpType
+
+P = 128
+PACK = 4
+PAIR = 2
+HALVES = PACK // PAIR
+K_PASS = P * PACK
+TOKENS = 1024
+TOKEN_TILES = TOKENS // P
+E = 2048
+D = 256
+HEAD_P = D // PACK
+EPS = 1e-5
+PASSES = E // K_PASS
+N_TILE = 512
+ROUND_PASSES = 2
+ROUND_K = ROUND_PASSES * K_PASS
+ROUND_HEADS = ROUND_K // D
+TILE_ROUNDS = PASSES // ROUND_PASSES
+ROUNDS = TOKEN_TILES * TILE_ROUNDS
+WORDS = ROUND_PASSES * P
+W_COLS = 1024
+W_PIECES = (E // W_COLS) * PASSES
+PIECES_PER_STEP = 2
+RAW_PIECES = 4
+UNIT_TILES = W_COLS // N_TILE
+UNITS = TOKEN_TILES * (E // W_COLS)
+STATS_AHEAD = 3
+UNIT_LAG = 3
+VECTOR_COLS = 512
+
+FLOPS = 2 * TOKENS * E * E
+
+
+def tile_multiscaleretention_pc_kernel(tc, ret, g, gn_weight, gn_bias, w_o, b_o, out):
+    nc = tc.nc
+    ret_rows = ret.flatten_outer_dims()
+    g_rows = g.flatten_outer_dims()
+    out_rows = out.flatten_outer_dims()
+    w_view = w_o.rearrange("(c p t) n -> c p t n", p=P, t=PACK)
+
+    with ExitStack() as ctx:
+        consts = ctx.enter_context(tc.tile_pool(name="consts", bufs=1))
+        keep = ctx.enter_context(tc.tile_pool(name="keep", bufs=1))
+        token_pool = ctx.enter_context(tc.tile_pool(name="token_pool", bufs=TOKEN_TILES))
+        norm_pool = ctx.enter_context(tc.tile_pool(name="norm_pool", bufs=3))
+        small = ctx.enter_context(tc.tile_pool(name="small", bufs=STATS_AHEAD + 2))
+        kmajor = ctx.enter_context(tc.tile_pool(name="kmajor", bufs=2))
+        w_raw_pool = ctx.enter_context(tc.tile_pool(name="w_raw_pool", bufs=RAW_PIECES))
+        w_grouped_pool = ctx.enter_context(tc.tile_pool(name="w_grouped_pool", bufs=3))
+        out_pool = ctx.enter_context(tc.tile_pool(name="out_pool", bufs=4))
+        psum_norm = ctx.enter_context(tc.psum_pool(name="psum_norm", bufs=3))
+        psum_g = ctx.enter_context(tc.psum_pool(name="psum_g", bufs=2))
+        psum_acc = ctx.enter_context(tc.psum_pool(name="psum_acc", bufs=3))
+        ctx.enter_context(tc.manual_schedule())
+
+        w_codes = keep.tile([P, PASSES, E], U32, align_bytes=64)
+        w_scales = keep.tile([P, PASSES, E], U8, align_bytes=64)
+        gate_codes = keep.tile([P, ROUNDS, WORDS], U32, align_bytes=64)
+        gate_scales = keep.tile([P, ROUNDS, WORDS], U8, align_bytes=64)
+
+        ret_tiles = {}
+        g_tiles = {}
+        raw_tiles = {}
+        grouped_tiles = {}
+
+        def load_tokens(rows_of, tiles, i, name):
+            if i < TOKEN_TILES:
+                tiles[i] = token_pool.tile([P, E], BF16, name=name)
+                nc.sync.dma_start(out=tiles[i][:], in_=rows_of[i * P : (i + 1) * P, :])
+
+        def load_w_piece(k):
+            if k < W_PIECES:
+                jj, c = divmod(k, PASSES)
+                raw_tiles[k] = w_raw_pool.tile([P, PACK, W_COLS], BF16, name="raw")
+                for u in range(HALVES):
+                    nc.sync.dma_start(
+                        out=raw_tiles[k][:, u * PAIR : (u + 1) * PAIR, :],
+                        in_=w_view[c, :, u * PAIR : (u + 1) * PAIR, jj * W_COLS : (jj + 1) * W_COLS],
+                    )
+
+        affine_rows = consts.tile([P, K_PASS], BF16)
+        nc.gpsimd.memset(affine_rows[:], 0.0)
+        load_tokens(ret_rows, ret_tiles, 0, "ret_t")
+        load_tokens(ret_rows, ret_tiles, 1, "ret_t")
+        load_tokens(g_rows, g_tiles, 0, "g_t")
+        nc.sync.dma_start(out=affine_rows[0:PASSES, :], in_=gn_weight.rearrange("(c x) -> c x", x=K_PASS))
+        nc.sync.dma_start(out=affine_rows[PASSES : 2 * PASSES, :], in_=gn_bias.rearrange("(c x) -> c x", x=K_PASS))
+        load_w_piece(0)
+        load_w_piece(1)
+        load_tokens(ret_rows, ret_tiles, 2, "ret_t")
+        load_w_piece(2)
+        load_w_piece(3)
+        load_tokens(g_rows, g_tiles, 1, "g_t")
+
+        ident_f32 = consts.tile([P, P], F32)
+        make_identity(nc, ident_f32[:])
+        neg_half = consts.tile([P, ROUND_HEADS], F32)
+        nc.gpsimd.memset(neg_half[:], -0.5)
+        bias_all = consts.tile([P, E], BF16)
+        affine_cols = consts.tile([P, HALVES, 2 * PASSES * PAIR], F32)
+
+        rstd_of = {}
+        shift_of = {}
+        norm_of = {}
+        norm_T_of = {}
+        g_T_of = {}
+        rn_T_of = {}
+        silu_T_of = {}
+        gate_grouped_of = {}
+
+        def statistics(n):
+            if n >= ROUNDS:
+                return
+            i, half = divmod(n, TILE_ROUNDS)
+            stats = small.tile([P, ROUND_HEADS, 3], F32, name="stats")
+            for first_head in range(0, ROUND_HEADS, 2):
+                first_col = half * ROUND_K + first_head * D
+                nc.vector.bn_stats(
+                    out=stats[:, first_head : first_head + 2, :].rearrange("p h s -> p (h s)"),
+                    in_=ret_tiles[i][:, first_col : first_col + 2 * D].rearrange("p (h d) -> p d h", h=2),
+                )
+            neg_mean = small.tile([P, ROUND_HEADS], F32, name="neg_mean")
+            nc.gpsimd.tensor_scalar(
+                out=neg_mean[:], in0=stats[:, :, 1], scalar1=-1.0, scalar2=0.0, op0=ALU.mult, op1=ALU.add
+            )
+            var_eps = small.tile([P, ROUND_HEADS], F32, name="var_eps")
+            nc.gpsimd.tensor_scalar(
+                out=var_eps[:], in0=stats[:, :, 2], scalar1=1.0 / D, scalar2=EPS, op0=ALU.mult, op1=ALU.add
+            )
+            rstd = small.tile([P, ROUND_HEADS], F32, name="rstd")
+            nc.gpsimd.tensor_tensor(out=rstd[:], in0=var_eps[:], in1=neg_half[:], op=ALU.pow)
+            shift = small.tile([P, ROUND_HEADS], F32, name="shift")
+            nc.gpsimd.tensor_tensor(out=shift[:], in0=neg_mean[:], in1=rstd[:], op=ALU.mult)
+            rstd_of[n] = rstd
+            shift_of[n] = shift
+
+        def normalise(n):
+            if n >= ROUNDS:
+                return
+            i, half = divmod(n, TILE_ROUNDS)
+            norm = norm_pool.tile([P, ROUND_PASSES, PACK, P], F32, name="norm")
+            for h in range(ROUND_HEADS):
+                first_col = half * ROUND_K + h * D
+                cr, hh = divmod(h, 2)
+                nc.scalar.activation(
+                    out=norm[:, cr, :, hh * HEAD_P : (hh + 1) * HEAD_P],
+                    in_=ret_tiles[i][:, first_col : first_col + D].rearrange("p (q t) -> p t q", t=PACK),
+                    func=ACT.Identity,
+                    scale=rstd_of[n][:, h : h + 1],
+                    bias=shift_of[n][:, h : h + 1],
+                )
+            norm_of[n] = norm
+
+        def transposes(n):
+            if n >= ROUNDS:
+                return
+            i, half = divmod(n, TILE_ROUNDS)
+            norm_T = [psum_norm.tile([P, PACK, P], F32, name="norm_T%d" % cr, tag="norm_T") for cr in range(ROUND_PASSES)]
+            for cr in range(ROUND_PASSES):
+                for t in range(PACK):
+                    nc.tensor.transpose(norm_T[cr][:, t, :], norm_of[n][:, cr, t, :], ident_f32[:])
+            g_T = psum_g.tile([P, HALVES * WORDS], F32, name="g_T")
+            g_words = g_tiles[i][:].bitcast(F32)
+            for u in range(HALVES):
+                for cr in range(ROUND_PASSES):
+                    first_word = (half * ROUND_K + cr * K_PASS) // PAIR
+                    nc.tensor.transpose(
+                        g_T[:, u * WORDS + cr * P : u * WORDS + (cr + 1) * P],
+                        g_words[:, first_word + u : first_word + K_PASS // PAIR : HALVES],
+                        ident_f32[:],
+                    )
+            norm_T_of[n] = norm_T
+            g_T_of[n] = g_T
+
+        def affine_and_silu(n):
+            if n >= ROUNDS:
+                return
+            half = n % TILE_ROUNDS
+            rn_T = kmajor.tile([P, PACK, WORDS], F32, name="rn_T")
+            for cr in range(ROUND_PASSES):
+                for t in range(PACK):
+                    u, e = divmod(t, PAIR)
+                    w_col = (half * ROUND_PASSES + cr) * PAIR + e
+                    b_col = PASSES * PAIR + w_col
+                    nc.scalar.activation(
+                        out=rn_T[:, t, cr * P : (cr + 1) * P], in_=norm_T_of[n][cr][:, t, :], func=ACT.Identity,
+                        scale=affine_cols[:, u, w_col : w_col + 1], bias=affine_cols[:, u, b_col : b_col + 1],
+                    )
+            silu_T = kmajor.tile([P, PACK, WORDS], F32, name="silu_T")
+            nc.scalar.activation(
+                out=silu_T[:].rearrange("p (u e) x -> p u e x", e=PAIR),
+                in_=g_T_of[n][:].bitcast(BF16).rearrange("p (u x e) -> p u e x", u=HALVES, e=PAIR),
+                func=ACT.Silu,
+            )
+            rn_T_of[n] = rn_T
+            silu_T_of[n] = silu_T
+
+        def gate_product(n):
+            if n < 0 or n >= ROUNDS:
+                return
+            gate_grouped = kmajor.tile([P, WORDS, PACK], BF16, name="gate_grouped", align_bytes=64)
+            nc.vector.tensor_tensor(
+                out=gate_grouped[:].rearrange("p (n i) t -> p n t i", i=4),
+                in0=rn_T_of[n][:].rearrange("p t (n i) -> p n t i", i=4),
+                in1=silu_T_of[n][:].rearrange("p t (n i) -> p n t i", i=4),
+                op=ALU.mult,
+            )
+            gate_grouped_of[n] = gate_grouped
+
+        def quantise_gate(n):
+            if n < 0 or n >= ROUNDS:
+                return
+            nc.vector.quantize_mx(
+                out=gate_codes[:, n, :].bitcast(FP8X4),
+                scales=gate_scales[:, n, :],
+                in_=gate_grouped_of[n][:].rearrange("p x t -> p (x t)"),
+            )
+
+        def regroup_w_piece(k):
+            if k >= W_PIECES:
+                return
+            v = VECTOR_COLS
+            grouped = w_grouped_pool.tile([P, W_COLS, PACK], BF16, name="grouped", align_bytes=64)
+            nc.vector.tensor_copy(
+                out=grouped[:, 0:v, :].rearrange("p (n i) t -> p n t i", i=4),
+                in_=raw_tiles[k][:, :, 0:v].rearrange("p t (n i) -> p n t i", i=4),
+            )
+            nc.scalar.copy(
+                out=grouped[:, v:W_COLS, :].rearrange("p (n i) t -> p n t i", i=4),
+                in_=raw_tiles[k][:, :, v:W_COLS].rearrange("p t (n i) -> p n t i", i=4),
+            )
+            grouped_tiles[k] = grouped
+
+        def quantise_w_piece(k):
+            if k < 0 or k >= W_PIECES:
+                return
+            jj, c = divmod(k, PASSES)
+            n_cols = slice(jj * W_COLS, (jj + 1) * W_COLS)
+            nc.vector.quantize_mx(
+                out=w_codes[:, c, n_cols].bitcast(FP8X4),
+                scales=w_scales[:, c, n_cols],
+                in_=grouped_tiles[k][:].rearrange("p n t -> p (n t)"),
+            )
+
+        def multiply(m):
+            if m < 0 or m >= UNITS:
+                return []
+            i, jj = divmod(m, E // W_COLS)
+            products = []
+            for j in range(jj * UNIT_TILES, (jj + 1) * UNIT_TILES):
+                n_cols = slice(j * N_TILE, (j + 1) * N_TILE)
+                acc = psum_acc.tile([P, N_TILE], F32, name="acc")
+                for c in range(PASSES):
+                    half, cr = divmod(c, ROUND_PASSES)
+                    made_in = i * TILE_ROUNDS + half
+                    nc.tensor.matmul_mx(
+                        out=acc[:],
+                        lhsT=gate_codes[:, made_in, cr * P : (cr + 1) * P].bitcast(FP8X4),
+                        lhsT_scale=gate_scales[:, made_in, cr * P : (cr + 1) * P],
+                        rhs=w_codes[:, c, n_cols].bitcast(FP8X4),
+                        rhs_scale=w_scales[:, c, n_cols],
+                        start=(c == 0),
+                        stop=(c == PASSES - 1),
+                    )
+                products.append((acc, slice(i * P, (i + 1) * P), n_cols))
+            return products
+
+        def add_bias_and_store(products):
+            for acc, tokens, n_cols in products:
+                result = out_pool.tile([P, N_TILE], F32, name="result")
+                nc.vector.tensor_tensor(out=result[:], in0=acc[:], in1=bias_all[:, n_cols], op=ALU.add)
+                nc.sync.dma_start(out=out_rows[tokens, n_cols], in_=result[:])
+
+        for n in range(STATS_AHEAD):
+            statistics(n)
+        affine_ps = psum_g.tile([P, HALVES * WORDS], F32, tag="g_T")
+        for u in range(HALVES):
+            nc.tensor.transpose(affine_ps[:, u * P : (u + 1) * P], affine_rows[:].bitcast(F32)[:, u::HALVES], ident_f32[:])
+        nc.vector.tensor_copy(
+            out=affine_cols[:],
+            in_=affine_ps[:, 0 : HALVES * P].bitcast(BF16).rearrange("p (u x) -> p u x", u=HALVES)[:, :, 0 : 2 * PASSES * PAIR],
+        )
+        normalise(0)
+
+        products = []
+        for n in range(ROUNDS + UNIT_LAG + 1):
+            statistics(n + STATS_AHEAD)
+            transposes(n)
+            normalise(n + 1)
+            affine_and_silu(n)
+            gate_product(n - 1)
+            add_bias_and_store(products)
+            quantise_gate(n - 1)
+            first = n * PIECES_PER_STEP
+            for k in range(first - PIECES_PER_STEP, first):
+                quantise_w_piece(k)
+            for k in range(first, first + PIECES_PER_STEP):
+                regroup_w_piece(k)
+            for k in range(first + RAW_PIECES, first + RAW_PIECES + PIECES_PER_STEP):
+                load_w_piece(k)
+            load_tokens(ret_rows, ret_tiles, n + 3, "ret_t")
+            load_tokens(g_rows, g_tiles, n + 2, "g_t")
+            if n == 1:
+                nc.sync.dma_start(out=bias_all[:], in_=b_o.partition_broadcast(P))
+            products = multiply(n - UNIT_LAG)

@@ -32,13 +32,14 @@ ROUNDS = TOKEN_TILES * TILE_ROUNDS
 WORDS = ROUND_PASSES * P
 W_COLS = 1024
 W_PIECES = (E // W_COLS) * PASSES
+FIRST_PIECES = 1
 PIECES_PER_STEP = 2
 RAW_PIECES = 4
 UNIT_TILES = W_COLS // N_TILE
 UNITS = TOKEN_TILES * (E // W_COLS)
 STATS_AHEAD = 3
-UNIT_LAG = 3
-VECTOR_COLS = 512
+MX_LAG = 3
+PS_COLS = 256
 
 FLOPS = 2 * TOKENS * E * E
 
@@ -59,10 +60,10 @@ def tile_multiscaleretention_pc_kernel(tc, ret, g, gn_weight, gn_bias, w_o, b_o,
         kmajor = ctx.enter_context(tc.tile_pool(name="kmajor", bufs=2))
         w_raw_pool = ctx.enter_context(tc.tile_pool(name="w_raw_pool", bufs=RAW_PIECES))
         w_grouped_pool = ctx.enter_context(tc.tile_pool(name="w_grouped_pool", bufs=3))
-        out_pool = ctx.enter_context(tc.tile_pool(name="out_pool", bufs=4))
-        psum_norm = ctx.enter_context(tc.psum_pool(name="psum_norm", bufs=3))
+        out_pool = ctx.enter_context(tc.tile_pool(name="out_pool", bufs=8))
+        psum_norm = ctx.enter_context(tc.psum_pool(name="psum_norm", bufs=2))
         psum_g = ctx.enter_context(tc.psum_pool(name="psum_g", bufs=2))
-        psum_acc = ctx.enter_context(tc.psum_pool(name="psum_acc", bufs=3))
+        psum_acc = ctx.enter_context(tc.psum_pool(name="psum_acc", bufs=4))
         ctx.enter_context(tc.manual_schedule())
 
         w_codes = keep.tile([P, PASSES, E], U32, align_bytes=64)
@@ -74,6 +75,7 @@ def tile_multiscaleretention_pc_kernel(tc, ret, g, gn_weight, gn_bias, w_o, b_o,
         g_tiles = {}
         raw_tiles = {}
         grouped_tiles = {}
+        banks_of = {}
 
         def load_tokens(rows_of, tiles, i, name):
             if i < TOKEN_TILES:
@@ -93,21 +95,23 @@ def tile_multiscaleretention_pc_kernel(tc, ret, g, gn_weight, gn_bias, w_o, b_o,
         affine_rows = consts.tile([P, K_PASS], BF16)
         nc.gpsimd.memset(affine_rows[:], 0.0)
         load_tokens(ret_rows, ret_tiles, 0, "ret_t")
-        load_tokens(ret_rows, ret_tiles, 1, "ret_t")
+        load_w_piece(0)
         load_tokens(g_rows, g_tiles, 0, "g_t")
         nc.sync.dma_start(out=affine_rows[0:PASSES, :], in_=gn_weight.rearrange("(c x) -> c x", x=K_PASS))
         nc.sync.dma_start(out=affine_rows[PASSES : 2 * PASSES, :], in_=gn_bias.rearrange("(c x) -> c x", x=K_PASS))
-        load_w_piece(0)
         load_w_piece(1)
-        load_tokens(ret_rows, ret_tiles, 2, "ret_t")
+        load_tokens(ret_rows, ret_tiles, 1, "ret_t")
         load_w_piece(2)
         load_w_piece(3)
-        load_tokens(g_rows, g_tiles, 1, "g_t")
 
-        ident_f32 = consts.tile([P, P], F32)
-        make_identity(nc, ident_f32[:])
         neg_half = consts.tile([P, ROUND_HEADS], F32)
         nc.gpsimd.memset(neg_half[:], -0.5)
+        first_silu = consts.tile([P, 1], F32)
+        nc.scalar.activation(out=first_silu[:], in_=neg_half[:, 0:1], func=ACT.Silu)
+        ident_f32 = consts.tile([P, P], F32)
+        make_identity(nc, ident_f32[:])
+        ident_bf16 = consts.tile([P, P], BF16)
+        make_identity(nc, ident_bf16[:])
         bias_all = consts.tile([P, E], BF16)
         affine_cols = consts.tile([P, HALVES, 2 * PASSES * PAIR], F32)
 
@@ -228,41 +232,62 @@ def tile_multiscaleretention_pc_kernel(tc, ret, g, gn_weight, gn_bias, w_o, b_o,
                 in_=gate_grouped_of[n][:].rearrange("p x t -> p (x t)"),
             )
 
-        def regroup_w_piece(k):
+        def regroup_w_on_vector(k):
             if k >= W_PIECES:
                 return
-            v = VECTOR_COLS
-            grouped = w_grouped_pool.tile([P, W_COLS, PACK], BF16, name="grouped", align_bytes=64)
+            grouped = w_grouped_pool.tile([P, N_TILE, PACK], BF16, name="grouped_v", align_bytes=64)
             nc.vector.tensor_copy(
-                out=grouped[:, 0:v, :].rearrange("p (n i) t -> p n t i", i=4),
-                in_=raw_tiles[k][:, :, 0:v].rearrange("p t (n i) -> p n t i", i=4),
+                out=grouped[:].rearrange("p (n i) t -> p n t i", i=4),
+                in_=raw_tiles[k][:, :, 0:N_TILE].rearrange("p t (n i) -> p n t i", i=4),
             )
-            nc.scalar.copy(
-                out=grouped[:, v:W_COLS, :].rearrange("p (n i) t -> p n t i", i=4),
-                in_=raw_tiles[k][:, :, v:W_COLS].rearrange("p t (n i) -> p n t i", i=4),
-            )
-            grouped_tiles[k] = grouped
+            grouped_tiles[k, 0] = grouped
 
-        def quantise_w_piece(k):
+        def regroup_w_on_tensor(k):
+            if k >= W_PIECES:
+                return
+            banks_of[k] = []
+            for first_col in range(N_TILE, W_COLS, PS_COLS):
+                bank = psum_acc.tile([P, PS_COLS, PACK], BF16, name="bank", tag="acc")
+                for x in range(0, PS_COLS, P):
+                    nc.tensor.matmul(
+                        out=bank[:, x : x + P, :],
+                        lhsT=ident_bf16[:],
+                        rhs=raw_tiles[k][:, :, first_col + x : first_col + x + P].rearrange("p t n -> p n t"),
+                        start=True,
+                        stop=True,
+                    )
+                banks_of[k].append(bank)
+
+        def copy_w_on_scalar(k):
+            if k >= W_PIECES:
+                return
+            grouped = w_grouped_pool.tile([P, N_TILE, PACK], BF16, name="grouped_s", align_bytes=64)
+            for x, bank in enumerate(banks_of[k]):
+                nc.scalar.copy(out=grouped[:, x * PS_COLS : (x + 1) * PS_COLS, :], in_=bank[:])
+            grouped_tiles[k, 1] = grouped
+
+        def quantise_w(k, part):
             if k < 0 or k >= W_PIECES:
                 return
             jj, c = divmod(k, PASSES)
-            n_cols = slice(jj * W_COLS, (jj + 1) * W_COLS)
+            n_cols = slice(jj * W_COLS + part * N_TILE, jj * W_COLS + (part + 1) * N_TILE)
             nc.vector.quantize_mx(
                 out=w_codes[:, c, n_cols].bitcast(FP8X4),
                 scales=w_scales[:, c, n_cols],
-                in_=grouped_tiles[k][:].rearrange("p n t -> p (n t)"),
+                in_=grouped_tiles[k, part][:].rearrange("p n t -> p (n t)"),
             )
 
-        def multiply(m):
-            if m < 0 or m >= UNITS:
-                return []
-            i, jj = divmod(m, E // W_COLS)
-            products = []
-            for j in range(jj * UNIT_TILES, (jj + 1) * UNIT_TILES):
+        def open_sums(i, columns, pool=None, tag="acc"):
+            sums = []
+            for j in columns:
+                acc = (pool or psum_acc).tile([P, N_TILE], F32, name="acc", tag=tag)
+                sums.append((acc, i, j))
+            return sums
+
+        def multiply(sums, passes):
+            for acc, i, j in sums:
                 n_cols = slice(j * N_TILE, (j + 1) * N_TILE)
-                acc = psum_acc.tile([P, N_TILE], F32, name="acc")
-                for c in range(PASSES):
+                for c in passes:
                     half, cr = divmod(c, ROUND_PASSES)
                     made_in = i * TILE_ROUNDS + half
                     nc.tensor.matmul_mx(
@@ -274,17 +299,23 @@ def tile_multiscaleretention_pc_kernel(tc, ret, g, gn_weight, gn_bias, w_o, b_o,
                         start=(c == 0),
                         stop=(c == PASSES - 1),
                     )
-                products.append((acc, slice(i * P, (i + 1) * P), n_cols))
-            return products
 
-        def add_bias_and_store(products):
-            for acc, tokens, n_cols in products:
+        def add_bias_and_store(sums):
+            for acc, i, j in sums:
+                n_cols = slice(j * N_TILE, (j + 1) * N_TILE)
                 result = out_pool.tile([P, N_TILE], F32, name="result")
                 nc.vector.tensor_tensor(out=result[:], in0=acc[:], in1=bias_all[:, n_cols], op=ALU.add)
-                nc.sync.dma_start(out=out_rows[tokens, n_cols], in_=result[:])
+                nc.sync.dma_start(out=out_rows[i * P : (i + 1) * P, n_cols], in_=result[:])
 
-        for n in range(STATS_AHEAD):
+        for n in range(TILE_ROUNDS):
             statistics(n)
+        for k in range(FIRST_PIECES):
+            regroup_w_on_tensor(k)
+            regroup_w_on_vector(k)
+            copy_w_on_scalar(k)
+            load_w_piece(k + RAW_PIECES)
+        load_tokens(ret_rows, ret_tiles, 2, "ret_t")
+        load_tokens(g_rows, g_tiles, 1, "g_t")
         affine_ps = psum_g.tile([P, HALVES * WORDS], F32, tag="g_T")
         for u in range(HALVES):
             nc.tensor.transpose(affine_ps[:, u * P : (u + 1) * P], affine_rows[:].bitcast(F32)[:, u::HALVES], ident_f32[:])
@@ -293,25 +324,48 @@ def tile_multiscaleretention_pc_kernel(tc, ret, g, gn_weight, gn_bias, w_o, b_o,
             in_=affine_ps[:, 0 : HALVES * P].bitcast(BF16).rearrange("p (u x) -> p u x", u=HALVES)[:, :, 0 : 2 * PASSES * PAIR],
         )
         normalise(0)
+        for k in range(FIRST_PIECES):
+            quantise_w(k, 0)
+        for n in range(TILE_ROUNDS, STATS_AHEAD):
+            statistics(n)
 
-        products = []
-        for n in range(ROUNDS + UNIT_LAG + 1):
-            statistics(n + STATS_AHEAD)
+        sums = []
+        for n in range(ROUNDS + 1):
+            first = FIRST_PIECES + n * PIECES_PER_STEP
             transposes(n)
+            statistics(n + STATS_AHEAD)
             normalise(n + 1)
             affine_and_silu(n)
+            for k in (first, first + 1):
+                regroup_w_on_tensor(k)
+                copy_w_on_scalar(k)
+            regroup_w_on_vector(first)
+            quantise_w(first - 2, 1)
+            quantise_w(first, 0)
             gate_product(n - 1)
-            add_bias_and_store(products)
+            regroup_w_on_vector(first + 1)
+            quantise_w(first - 1, 1)
             quantise_gate(n - 1)
-            first = n * PIECES_PER_STEP
-            for k in range(first - PIECES_PER_STEP, first):
-                quantise_w_piece(k)
-            for k in range(first, first + PIECES_PER_STEP):
-                regroup_w_piece(k)
-            for k in range(first + RAW_PIECES, first + RAW_PIECES + PIECES_PER_STEP):
-                load_w_piece(k)
-            load_tokens(ret_rows, ret_tiles, n + 3, "ret_t")
-            load_tokens(g_rows, g_tiles, n + 2, "g_t")
+            quantise_w(first + 1, 0)
+            add_bias_and_store(sums)
+            load_w_piece(first + RAW_PIECES)
+            load_w_piece(first + RAW_PIECES + 1)
+            if n > 0:
+                load_tokens(ret_rows, ret_tiles, n + 2, "ret_t")
+                load_tokens(g_rows, g_tiles, n + 1, "g_t")
             if n == 1:
                 nc.sync.dma_start(out=bias_all[:], in_=b_o.partition_broadcast(P))
-            products = multiply(n - UNIT_LAG)
+            sums = []
+            for i in range(TOKEN_TILES - 1):
+                for j in range(E // N_TILE):
+                    if n == TILE_ROUNDS * i + MX_LAG + j // 2:
+                        block = open_sums(i, [j])
+                        multiply(block, range(PASSES))
+                        sums += block
+            if n == ROUNDS:
+                last = open_sums(TOKEN_TILES - 1, (0, 1), psum_norm, "norm_T")
+                last += open_sums(TOKEN_TILES - 1, (2, 3))
+                multiply(last, range(ROUND_PASSES))
+                multiply(last, range(ROUND_PASSES, PASSES))
+                sums += last
+        add_bias_and_store(sums)

@@ -39,7 +39,6 @@ UNIT_TILES = W_COLS // N_TILE
 UNITS = TOKEN_TILES * (E // W_COLS)
 STATS_AHEAD = 3
 MX_LAG = 3
-PS_COLS = 256
 
 FLOPS = 2 * TOKENS * E * E
 
@@ -75,7 +74,6 @@ def tile_multiscaleretention_pc_kernel(tc, ret, g, gn_weight, gn_bias, w_o, b_o,
         g_tiles = {}
         raw_tiles = {}
         grouped_tiles = {}
-        banks_of = {}
 
         def load_tokens(rows_of, tiles, i, name):
             if i < TOKEN_TILES:
@@ -110,8 +108,6 @@ def tile_multiscaleretention_pc_kernel(tc, ret, g, gn_weight, gn_bias, w_o, b_o,
         nc.scalar.activation(out=first_silu[:], in_=neg_half[:, 0:1], func=ACT.Silu)
         ident_f32 = consts.tile([P, P], F32)
         make_identity(nc, ident_f32[:])
-        ident_bf16 = consts.tile([P, P], BF16)
-        make_identity(nc, ident_bf16[:])
         bias_all = consts.tile([P, E], BF16)
         affine_cols = consts.tile([P, HALVES, 2 * PASSES * PAIR], F32)
 
@@ -242,28 +238,14 @@ def tile_multiscaleretention_pc_kernel(tc, ret, g, gn_weight, gn_bias, w_o, b_o,
             )
             grouped_tiles[k, 0] = grouped
 
-        def regroup_w_on_tensor(k):
-            if k >= W_PIECES:
-                return
-            banks_of[k] = []
-            for first_col in range(N_TILE, W_COLS, PS_COLS):
-                bank = psum_acc.tile([P, PS_COLS, PACK], BF16, name="bank", tag="acc")
-                for x in range(0, PS_COLS, P):
-                    nc.tensor.matmul(
-                        out=bank[:, x : x + P, :],
-                        lhsT=ident_bf16[:],
-                        rhs=raw_tiles[k][:, :, first_col + x : first_col + x + P].rearrange("p t n -> p n t"),
-                        start=True,
-                        stop=True,
-                    )
-                banks_of[k].append(bank)
-
-        def copy_w_on_scalar(k):
+        def regroup_w_on_scalar(k):
             if k >= W_PIECES:
                 return
             grouped = w_grouped_pool.tile([P, N_TILE, PACK], BF16, name="grouped_s", align_bytes=64)
-            for x, bank in enumerate(banks_of[k]):
-                nc.scalar.copy(out=grouped[:, x * PS_COLS : (x + 1) * PS_COLS, :], in_=bank[:])
+            nc.scalar.copy(
+                out=grouped[:].rearrange("p (n i) t -> p n t i", i=4),
+                in_=raw_tiles[k][:, :, N_TILE:W_COLS].rearrange("p t (n i) -> p n t i", i=4),
+            )
             grouped_tiles[k, 1] = grouped
 
         def quantise_w(k, part):
@@ -310,9 +292,8 @@ def tile_multiscaleretention_pc_kernel(tc, ret, g, gn_weight, gn_bias, w_o, b_o,
         for n in range(TILE_ROUNDS):
             statistics(n)
         for k in range(FIRST_PIECES):
-            regroup_w_on_tensor(k)
             regroup_w_on_vector(k)
-            copy_w_on_scalar(k)
+            regroup_w_on_scalar(k)
             load_w_piece(k + RAW_PIECES)
         load_tokens(ret_rows, ret_tiles, 2, "ret_t")
         load_tokens(g_rows, g_tiles, 1, "g_t")
@@ -337,8 +318,7 @@ def tile_multiscaleretention_pc_kernel(tc, ret, g, gn_weight, gn_bias, w_o, b_o,
             normalise(n + 1)
             affine_and_silu(n)
             for k in (first, first + 1):
-                regroup_w_on_tensor(k)
-                copy_w_on_scalar(k)
+                regroup_w_on_scalar(k)
             regroup_w_on_vector(first)
             quantise_w(first - 2, 1)
             quantise_w(first, 0)

@@ -23,6 +23,7 @@ D = 256
 HEAD_P = D // PACK
 EPS = 1e-5
 PASSES = E // K_PASS
+HEADS = E // D
 N_TILE = 512
 ROUND_PASSES = 2
 ROUND_K = ROUND_PASSES * K_PASS
@@ -37,7 +38,7 @@ PIECES_PER_STEP = 2
 RAW_PIECES = 4
 UNIT_TILES = W_COLS // N_TILE
 UNITS = TOKEN_TILES * (E // W_COLS)
-STATS_AHEAD = 3
+STATS_AHEAD = 4
 MX_LAG = 3
 
 FLOPS = 2 * TOKENS * E * E
@@ -97,12 +98,13 @@ def tile_multiscaleretention_pc_kernel(tc, ret, g, gn_weight, gn_bias, w_o, b_o,
         load_tokens(g_rows, g_tiles, 0, "g_t")
         nc.sync.dma_start(out=affine_rows[0:PASSES, :], in_=gn_weight.rearrange("(c x) -> c x", x=K_PASS))
         nc.sync.dma_start(out=affine_rows[PASSES : 2 * PASSES, :], in_=gn_bias.rearrange("(c x) -> c x", x=K_PASS))
-        load_w_piece(1)
         load_tokens(ret_rows, ret_tiles, 1, "ret_t")
+        load_w_piece(1)
+        load_tokens(ret_rows, ret_tiles, 2, "ret_t")
         load_w_piece(2)
         load_w_piece(3)
 
-        neg_half = consts.tile([P, ROUND_HEADS], F32)
+        neg_half = consts.tile([P, HEADS], F32)
         nc.gpsimd.memset(neg_half[:], -0.5)
         first_silu = consts.tile([P, 1], F32)
         nc.scalar.activation(out=first_silu[:], in_=neg_half[:, 0:1], func=ACT.Silu)
@@ -111,6 +113,7 @@ def tile_multiscaleretention_pc_kernel(tc, ret, g, gn_weight, gn_bias, w_o, b_o,
         bias_all = consts.tile([P, E], BF16)
         affine_cols = consts.tile([P, HALVES, 2 * PASSES * PAIR], F32)
 
+        stats_of = {}
         rstd_of = {}
         shift_of = {}
         norm_of = {}
@@ -120,31 +123,35 @@ def tile_multiscaleretention_pc_kernel(tc, ret, g, gn_weight, gn_bias, w_o, b_o,
         silu_T_of = {}
         gate_grouped_of = {}
 
-        def statistics(n):
+        def head_sums(n):
             if n >= ROUNDS:
                 return
             i, half = divmod(n, TILE_ROUNDS)
-            stats = small.tile([P, ROUND_HEADS, 3], F32, name="stats")
-            for first_head in range(0, ROUND_HEADS, 2):
-                first_col = half * ROUND_K + first_head * D
+            if half == 0:
+                stats_of[i] = small.tile([P, HEADS, 3], F32, name="stats")
+            for first_head in range(half * ROUND_HEADS, (half + 1) * ROUND_HEADS, 2):
                 nc.vector.bn_stats(
-                    out=stats[:, first_head : first_head + 2, :].rearrange("p h s -> p (h s)"),
-                    in_=ret_tiles[i][:, first_col : first_col + 2 * D].rearrange("p (h d) -> p d h", h=2),
+                    out=stats_of[i][:, first_head : first_head + 2, :].rearrange("p h s -> p (h s)"),
+                    in_=ret_tiles[i][:, first_head * D : (first_head + 2) * D].rearrange("p (h d) -> p d h", h=2),
                 )
-            neg_mean = small.tile([P, ROUND_HEADS], F32, name="neg_mean")
-            nc.gpsimd.tensor_scalar(
-                out=neg_mean[:], in0=stats[:, :, 1], scalar1=-1.0, scalar2=0.0, op0=ALU.mult, op1=ALU.add
+
+        def reciprocal_deviations(i):
+            if i >= TOKEN_TILES:
+                return
+            var_eps = small.tile([P, HEADS], F32, name="var_eps")
+            nc.vector.tensor_scalar(
+                out=var_eps[:], in0=stats_of[i][:, :, 2], scalar1=1.0 / D, scalar2=EPS, op0=ALU.mult, op1=ALU.add
             )
-            var_eps = small.tile([P, ROUND_HEADS], F32, name="var_eps")
-            nc.gpsimd.tensor_scalar(
-                out=var_eps[:], in0=stats[:, :, 2], scalar1=1.0 / D, scalar2=EPS, op0=ALU.mult, op1=ALU.add
+            rstd_of[i] = small.tile([P, HEADS], F32, name="rstd")
+            nc.gpsimd.tensor_tensor(out=rstd_of[i][:], in0=var_eps[:], in1=neg_half[:], op=ALU.pow)
+
+        def shifts(i):
+            if i >= TOKEN_TILES:
+                return
+            shift_of[i] = small.tile([P, HEADS], F32, name="shift")
+            nc.vector.scalar_tensor_tensor(
+                out=shift_of[i][:], in0=stats_of[i][:, :, 1], scalar=-1.0, in1=rstd_of[i][:], op0=ALU.mult, op1=ALU.mult
             )
-            rstd = small.tile([P, ROUND_HEADS], F32, name="rstd")
-            nc.gpsimd.tensor_tensor(out=rstd[:], in0=var_eps[:], in1=neg_half[:], op=ALU.pow)
-            shift = small.tile([P, ROUND_HEADS], F32, name="shift")
-            nc.gpsimd.tensor_tensor(out=shift[:], in0=neg_mean[:], in1=rstd[:], op=ALU.mult)
-            rstd_of[n] = rstd
-            shift_of[n] = shift
 
         def normalise(n):
             if n >= ROUNDS:
@@ -158,8 +165,8 @@ def tile_multiscaleretention_pc_kernel(tc, ret, g, gn_weight, gn_bias, w_o, b_o,
                     out=norm[:, cr, :, hh * HEAD_P : (hh + 1) * HEAD_P],
                     in_=ret_tiles[i][:, first_col : first_col + D].rearrange("p (q t) -> p t q", t=PACK),
                     func=ACT.Identity,
-                    scale=rstd_of[n][:, h : h + 1],
-                    bias=shift_of[n][:, h : h + 1],
+                    scale=rstd_of[i][:, half * ROUND_HEADS + h : half * ROUND_HEADS + h + 1],
+                    bias=shift_of[i][:, half * ROUND_HEADS + h : half * ROUND_HEADS + h + 1],
                 )
             norm_of[n] = norm
 
@@ -290,13 +297,14 @@ def tile_multiscaleretention_pc_kernel(tc, ret, g, gn_weight, gn_bias, w_o, b_o,
                 nc.sync.dma_start(out=out_rows[i * P : (i + 1) * P, n_cols], in_=result[:])
 
         for n in range(TILE_ROUNDS):
-            statistics(n)
+            head_sums(n)
+        reciprocal_deviations(0)
         for k in range(FIRST_PIECES):
             regroup_w_on_vector(k)
             regroup_w_on_scalar(k)
             load_w_piece(k + RAW_PIECES)
-        load_tokens(ret_rows, ret_tiles, 2, "ret_t")
         load_tokens(g_rows, g_tiles, 1, "g_t")
+        shifts(0)
         affine_ps = psum_g.tile([P, HALVES * WORDS], F32, tag="g_T")
         for u in range(HALVES):
             nc.tensor.transpose(affine_ps[:, u * P : (u + 1) * P], affine_rows[:].bitcast(F32)[:, u::HALVES], ident_f32[:])
@@ -305,34 +313,43 @@ def tile_multiscaleretention_pc_kernel(tc, ret, g, gn_weight, gn_bias, w_o, b_o,
             in_=affine_ps[:, 0 : HALVES * P].bitcast(BF16).rearrange("p (u x) -> p u x", u=HALVES)[:, :, 0 : 2 * PASSES * PAIR],
         )
         normalise(0)
+        for n in range(TILE_ROUNDS, STATS_AHEAD):
+            head_sums(n)
         for k in range(FIRST_PIECES):
             quantise_w(k, 0)
-        for n in range(TILE_ROUNDS, STATS_AHEAD):
-            statistics(n)
+        reciprocal_deviations(1)
 
         sums = []
         for n in range(ROUNDS + 1):
             first = FIRST_PIECES + n * PIECES_PER_STEP
+            ahead, odd = divmod(n + STATS_AHEAD, TILE_ROUNDS)
             transposes(n)
-            statistics(n + STATS_AHEAD)
             normalise(n + 1)
             affine_and_silu(n)
             for k in (first, first + 1):
                 regroup_w_on_scalar(k)
             regroup_w_on_vector(first)
             quantise_w(first - 2, 1)
-            quantise_w(first, 0)
             gate_product(n - 1)
+            quantise_w(first, 0)
+            if not odd:
+                shifts(ahead - 1)
             regroup_w_on_vector(first + 1)
-            quantise_w(first - 1, 1)
+            head_sums(n + STATS_AHEAD)
             quantise_gate(n - 1)
+            quantise_w(first - 1, 1)
             quantise_w(first + 1, 0)
+            if odd:
+                reciprocal_deviations(ahead)
             add_bias_and_store(sums)
             load_w_piece(first + RAW_PIECES)
             load_w_piece(first + RAW_PIECES + 1)
-            if n > 0:
-                load_tokens(ret_rows, ret_tiles, n + 2, "ret_t")
+            if n == 0:
+                load_tokens(ret_rows, ret_tiles, 3, "ret_t")
+            else:
                 load_tokens(g_rows, g_tiles, n + 1, "g_t")
+                if n > 1:
+                    load_tokens(ret_rows, ret_tiles, n + 2, "ret_t")
             if n == 1:
                 nc.sync.dma_start(out=bias_all[:], in_=b_o.partition_broadcast(P))
             sums = []

@@ -38,7 +38,6 @@ PIECES_PER_STEP = 2
 RAW_PIECES = 4
 UNIT_TILES = W_COLS // N_TILE
 UNITS = TOKEN_TILES * (E // W_COLS)
-STATS_AHEAD = 4
 MX_LAG = 3
 
 FLOPS = 2 * TOKENS * E * E
@@ -56,7 +55,7 @@ def tile_multiscaleretention_pc_kernel(tc, ret, g, gn_weight, gn_bias, w_o, b_o,
         keep = ctx.enter_context(tc.tile_pool(name="keep", bufs=1))
         token_pool = ctx.enter_context(tc.tile_pool(name="token_pool", bufs=TOKEN_TILES))
         norm_pool = ctx.enter_context(tc.tile_pool(name="norm_pool", bufs=3))
-        small = ctx.enter_context(tc.tile_pool(name="small", bufs=STATS_AHEAD + 2))
+        small = ctx.enter_context(tc.tile_pool(name="small", bufs=3))
         kmajor = ctx.enter_context(tc.tile_pool(name="kmajor", bufs=2))
         w_raw_pool = ctx.enter_context(tc.tile_pool(name="w_raw_pool", bufs=RAW_PIECES))
         w_grouped_pool = ctx.enter_context(tc.tile_pool(name="w_grouped_pool", bufs=3))
@@ -94,11 +93,11 @@ def tile_multiscaleretention_pc_kernel(tc, ret, g, gn_weight, gn_bias, w_o, b_o,
         affine_rows = consts.tile([P, K_PASS], BF16)
         nc.gpsimd.memset(affine_rows[:], 0.0)
         load_tokens(ret_rows, ret_tiles, 0, "ret_t")
+        load_tokens(ret_rows, ret_tiles, 1, "ret_t")
         load_w_piece(0)
         load_tokens(g_rows, g_tiles, 0, "g_t")
         nc.sync.dma_start(out=affine_rows[0:PASSES, :], in_=gn_weight.rearrange("(c x) -> c x", x=K_PASS))
         nc.sync.dma_start(out=affine_rows[PASSES : 2 * PASSES, :], in_=gn_bias.rearrange("(c x) -> c x", x=K_PASS))
-        load_tokens(ret_rows, ret_tiles, 1, "ret_t")
         load_w_piece(1)
         load_tokens(ret_rows, ret_tiles, 2, "ret_t")
         load_w_piece(2)
@@ -123,16 +122,14 @@ def tile_multiscaleretention_pc_kernel(tc, ret, g, gn_weight, gn_bias, w_o, b_o,
         silu_T_of = {}
         gate_grouped_of = {}
 
-        def head_sums(n):
-            if n >= ROUNDS:
+        def head_sums(i):
+            if i >= TOKEN_TILES:
                 return
-            i, half = divmod(n, TILE_ROUNDS)
-            if half == 0:
-                stats_of[i] = small.tile([P, HEADS, 3], F32, name="stats")
-            for first_head in range(half * ROUND_HEADS, (half + 1) * ROUND_HEADS, 2):
+            stats_of[i] = small.tile([P, HEADS, 3], F32, name="stats")
+            for h in range(0, HEADS, 2):
                 nc.vector.bn_stats(
-                    out=stats_of[i][:, first_head : first_head + 2, :].rearrange("p h s -> p (h s)"),
-                    in_=ret_tiles[i][:, first_head * D : (first_head + 2) * D].rearrange("p (h d) -> p d h", h=2),
+                    out=stats_of[i][:, h : h + 2, :].rearrange("p h s -> p (h s)"),
+                    in_=ret_tiles[i][:, h * D : (h + 2) * D].rearrange("p (h d) -> p d h", h=2),
                 )
 
         def reciprocal_deviations(i):
@@ -296,15 +293,16 @@ def tile_multiscaleretention_pc_kernel(tc, ret, g, gn_weight, gn_bias, w_o, b_o,
                 nc.vector.tensor_tensor(out=result[:], in0=acc[:], in1=bias_all[:, n_cols], op=ALU.add)
                 nc.sync.dma_start(out=out_rows[i * P : (i + 1) * P, n_cols], in_=result[:])
 
-        for n in range(TILE_ROUNDS):
-            head_sums(n)
+        head_sums(0)
         reciprocal_deviations(0)
+        head_sums(1)
+        shifts(0)
         for k in range(FIRST_PIECES):
             regroup_w_on_vector(k)
             regroup_w_on_scalar(k)
             load_w_piece(k + RAW_PIECES)
         load_tokens(g_rows, g_tiles, 1, "g_t")
-        shifts(0)
+        load_tokens(ret_rows, ret_tiles, 3, "ret_t")
         affine_ps = psum_g.tile([P, HALVES * WORDS], F32, tag="g_T")
         for u in range(HALVES):
             nc.tensor.transpose(affine_ps[:, u * P : (u + 1) * P], affine_rows[:].bitcast(F32)[:, u::HALVES], ident_f32[:])
@@ -313,16 +311,12 @@ def tile_multiscaleretention_pc_kernel(tc, ret, g, gn_weight, gn_bias, w_o, b_o,
             in_=affine_ps[:, 0 : HALVES * P].bitcast(BF16).rearrange("p (u x) -> p u x", u=HALVES)[:, :, 0 : 2 * PASSES * PAIR],
         )
         normalise(0)
-        for n in range(TILE_ROUNDS, STATS_AHEAD):
-            head_sums(n)
         for k in range(FIRST_PIECES):
             quantise_w(k, 0)
-        reciprocal_deviations(1)
 
         sums = []
         for n in range(ROUNDS + 1):
             first = FIRST_PIECES + n * PIECES_PER_STEP
-            ahead, odd = divmod(n + STATS_AHEAD, TILE_ROUNDS)
             transposes(n)
             normalise(n + 1)
             affine_and_silu(n)
@@ -332,21 +326,19 @@ def tile_multiscaleretention_pc_kernel(tc, ret, g, gn_weight, gn_bias, w_o, b_o,
             quantise_w(first - 2, 1)
             gate_product(n - 1)
             quantise_w(first, 0)
-            if not odd:
-                shifts(ahead - 1)
-            regroup_w_on_vector(first + 1)
-            head_sums(n + STATS_AHEAD)
+            add_bias_and_store(sums)
             quantise_gate(n - 1)
+            if n == 0 or n % TILE_ROUNDS == 1:
+                i = (n + 1) // TILE_ROUNDS + 1
+                reciprocal_deviations(i)
+                head_sums(i + 1)
+                shifts(i)
+            regroup_w_on_vector(first + 1)
             quantise_w(first - 1, 1)
             quantise_w(first + 1, 0)
-            if odd:
-                reciprocal_deviations(ahead)
-            add_bias_and_store(sums)
             load_w_piece(first + RAW_PIECES)
             load_w_piece(first + RAW_PIECES + 1)
-            if n == 0:
-                load_tokens(ret_rows, ret_tiles, 3, "ret_t")
-            else:
+            if n > 0:
                 load_tokens(g_rows, g_tiles, n + 1, "g_t")
                 if n > 1:
                     load_tokens(ret_rows, ret_tiles, n + 2, "ret_t")

@@ -326,13 +326,16 @@ def tile_multiscaleretention_pc_kernel(tc, ret, g, gn_weight, gn_bias, w_o, b_o,
             quantise_w(first - 2, 1)
             gate_product(n - 1)
             quantise_w(first, 0)
-            add_bias_and_store(sums)
-            quantise_gate(n - 1)
             if n == 0 or n % TILE_ROUNDS == 1:
                 i = (n + 1) // TILE_ROUNDS + 1
                 reciprocal_deviations(i)
+                add_bias_and_store(sums)
                 head_sums(i + 1)
                 shifts(i)
+                quantise_gate(n - 1)
+            else:
+                add_bias_and_store(sums)
+                quantise_gate(n - 1)
             regroup_w_on_vector(first + 1)
             quantise_w(first - 1, 1)
             quantise_w(first + 1, 0)

@@ -40,6 +40,11 @@ UNIT_TILES = W_COLS // N_TILE
 UNITS = TOKEN_TILES * (E // W_COLS)
 MX_LAG = 3
 
+PS_COLS = 256
+
+SCALAR_PIECES = (0, 2)
+LAST_ROUNDS = 3
+VECTOR_HEADS = 2
 FLOPS = 2 * TOKENS * E * E
 
 
@@ -57,9 +62,11 @@ def tile_multiscaleretention_pc_kernel(tc, ret, g, gn_weight, gn_bias, w_o, b_o,
         norm_pool = ctx.enter_context(tc.tile_pool(name="norm_pool", bufs=3))
         small = ctx.enter_context(tc.tile_pool(name="small", bufs=3))
         kmajor = ctx.enter_context(tc.tile_pool(name="kmajor", bufs=2))
+        parted_pool = ctx.enter_context(tc.tile_pool(name="parted_pool", bufs=2))
         w_raw_pool = ctx.enter_context(tc.tile_pool(name="w_raw_pool", bufs=RAW_PIECES))
-        w_grouped_pool = ctx.enter_context(tc.tile_pool(name="w_grouped_pool", bufs=3))
-        out_pool = ctx.enter_context(tc.tile_pool(name="out_pool", bufs=8))
+        grouped_v_pool = ctx.enter_context(tc.tile_pool(name="grouped_v_pool", bufs=2))
+        grouped_s_pool = ctx.enter_context(tc.tile_pool(name="grouped_s_pool", bufs=5))
+        out_pool = ctx.enter_context(tc.tile_pool(name="out_pool", bufs=6))
         psum_norm = ctx.enter_context(tc.psum_pool(name="psum_norm", bufs=2))
         psum_g = ctx.enter_context(tc.psum_pool(name="psum_g", bufs=2))
         psum_acc = ctx.enter_context(tc.psum_pool(name="psum_acc", bufs=4))
@@ -74,6 +81,7 @@ def tile_multiscaleretention_pc_kernel(tc, ret, g, gn_weight, gn_bias, w_o, b_o,
         g_tiles = {}
         raw_tiles = {}
         grouped_tiles = {}
+        banks_of = {}
 
         def load_tokens(rows_of, tiles, i, name):
             if i < TOKEN_TILES:
@@ -93,8 +101,8 @@ def tile_multiscaleretention_pc_kernel(tc, ret, g, gn_weight, gn_bias, w_o, b_o,
         affine_rows = consts.tile([P, K_PASS], BF16)
         nc.gpsimd.memset(affine_rows[:], 0.0)
         load_tokens(ret_rows, ret_tiles, 0, "ret_t")
-        load_tokens(ret_rows, ret_tiles, 1, "ret_t")
         load_w_piece(0)
+        load_tokens(ret_rows, ret_tiles, 1, "ret_t")
         load_tokens(g_rows, g_tiles, 0, "g_t")
         nc.sync.dma_start(out=affine_rows[0:PASSES, :], in_=gn_weight.rearrange("(c x) -> c x", x=K_PASS))
         nc.sync.dma_start(out=affine_rows[PASSES : 2 * PASSES, :], in_=gn_bias.rearrange("(c x) -> c x", x=K_PASS))
@@ -109,6 +117,8 @@ def tile_multiscaleretention_pc_kernel(tc, ret, g, gn_weight, gn_bias, w_o, b_o,
         nc.scalar.activation(out=first_silu[:], in_=neg_half[:, 0:1], func=ACT.Silu)
         ident_f32 = consts.tile([P, P], F32)
         make_identity(nc, ident_f32[:])
+        ident_bf16 = consts.tile([P, P], BF16)
+        make_identity(nc, ident_bf16[:])
         bias_all = consts.tile([P, E], BF16)
         affine_cols = consts.tile([P, HALVES, 2 * PASSES * PAIR], F32)
 
@@ -118,6 +128,7 @@ def tile_multiscaleretention_pc_kernel(tc, ret, g, gn_weight, gn_bias, w_o, b_o,
         norm_of = {}
         norm_T_of = {}
         g_T_of = {}
+        parted_of = {}
         rn_T_of = {}
         silu_T_of = {}
         gate_grouped_of = {}
@@ -150,12 +161,16 @@ def tile_multiscaleretention_pc_kernel(tc, ret, g, gn_weight, gn_bias, w_o, b_o,
                 out=shift_of[i][:], in0=stats_of[i][:, :, 1], scalar=-1.0, in1=rstd_of[i][:], op0=ALU.mult, op1=ALU.mult
             )
 
+        def vector_heads(n):
+            return VECTOR_HEADS if n >= ROUNDS - LAST_ROUNDS else 0
+
         def normalise(n):
             if n >= ROUNDS:
                 return
             i, half = divmod(n, TILE_ROUNDS)
             norm = norm_pool.tile([P, ROUND_PASSES, PACK, P], F32, name="norm")
-            for h in range(ROUND_HEADS):
+            norm_of[n] = norm
+            for h in range(vector_heads(n), ROUND_HEADS):
                 first_col = half * ROUND_K + h * D
                 cr, hh = divmod(h, 2)
                 nc.scalar.activation(
@@ -165,7 +180,29 @@ def tile_multiscaleretention_pc_kernel(tc, ret, g, gn_weight, gn_bias, w_o, b_o,
                     scale=rstd_of[i][:, half * ROUND_HEADS + h : half * ROUND_HEADS + h + 1],
                     bias=shift_of[i][:, half * ROUND_HEADS + h : half * ROUND_HEADS + h + 1],
                 )
-            norm_of[n] = norm
+
+        def normalise_on_vector(n):
+            if n >= ROUNDS:
+                return
+            i, half = divmod(n, TILE_ROUNDS)
+            for h in range(vector_heads(n)):
+                first_col = half * ROUND_K + h * D
+                cr, hh = divmod(h, 2)
+                nc.vector.tensor_scalar(
+                    out=norm_of[n][:, cr, :, hh * HEAD_P : (hh + 1) * HEAD_P],
+                    in0=ret_tiles[i][:, first_col : first_col + D].rearrange("p (q t) -> p t q", t=PACK),
+                    scalar1=rstd_of[i][:, half * ROUND_HEADS + h : half * ROUND_HEADS + h + 1],
+                    scalar2=shift_of[i][:, half * ROUND_HEADS + h : half * ROUND_HEADS + h + 1],
+                    op0=ALU.mult,
+                    op1=ALU.add,
+                )
+
+        def part_g(n):
+            if n >= ROUNDS or not (n >= ROUNDS - LAST_ROUNDS):
+                return
+            i, half = divmod(n, TILE_ROUNDS)
+            parted_of[n] = parted_pool.tile([P, ROUND_PASSES, HALVES, P], F32, name="parted")
+            nc.vector.tensor_copy(out=parted_of[n][:], in_=g_tiles[i][:].bitcast(F32)[:, half * ROUND_K // 2 : (half + 1) * ROUND_K // 2].rearrange("p (c q u) -> p c u q", c=ROUND_PASSES, u=HALVES))
 
         def transposes(n):
             if n >= ROUNDS:
@@ -177,6 +214,13 @@ def tile_multiscaleretention_pc_kernel(tc, ret, g, gn_weight, gn_bias, w_o, b_o,
                     nc.tensor.transpose(norm_T[cr][:, t, :], norm_of[n][:, cr, t, :], ident_f32[:])
             g_T = psum_g.tile([P, HALVES * WORDS], F32, name="g_T")
             g_words = g_tiles[i][:].bitcast(F32)
+            if n in parted_of:
+                for u in range(HALVES):
+                    for cr in range(ROUND_PASSES):
+                        nc.tensor.transpose(g_T[:, u * WORDS + cr * P : u * WORDS + (cr + 1) * P], parted_of[n][:, cr, u, :], ident_f32[:])
+                norm_T_of[n] = norm_T
+                g_T_of[n] = g_T
+                return
             for u in range(HALVES):
                 for cr in range(ROUND_PASSES):
                     first_word = (half * ROUND_K + cr * K_PASS) // PAIR
@@ -235,21 +279,43 @@ def tile_multiscaleretention_pc_kernel(tc, ret, g, gn_weight, gn_bias, w_o, b_o,
         def regroup_w_on_vector(k):
             if k >= W_PIECES:
                 return
-            grouped = w_grouped_pool.tile([P, N_TILE, PACK], BF16, name="grouped_v", align_bytes=64)
+            if k in SCALAR_PIECES:
+                return
+            grouped = grouped_v_pool.tile([P, N_TILE, PACK], BF16, name="grouped_v", align_bytes=64)
             nc.vector.tensor_copy(
                 out=grouped[:].rearrange("p (n i) t -> p n t i", i=4),
                 in_=raw_tiles[k][:, :, 0:N_TILE].rearrange("p t (n i) -> p n t i", i=4),
             )
             grouped_tiles[k, 0] = grouped
 
-        def regroup_w_on_scalar(k):
+        def regroup_w_on_tensor(k):
             if k >= W_PIECES:
                 return
-            grouped = w_grouped_pool.tile([P, N_TILE, PACK], BF16, name="grouped_s", align_bytes=64)
-            nc.scalar.copy(
-                out=grouped[:].rearrange("p (n i) t -> p n t i", i=4),
-                in_=raw_tiles[k][:, :, N_TILE:W_COLS].rearrange("p t (n i) -> p n t i", i=4),
-            )
+            banks_of[k] = []
+            for first_col in range(N_TILE, W_COLS, PS_COLS):
+                bank = psum_acc.tile([P, PS_COLS, PACK], BF16, name="bank", tag="acc")
+                for x in range(0, PS_COLS, P):
+                    nc.tensor.matmul(
+                        out=bank[:, x : x + P, :].rearrange("p (n i) t -> p n t i", i=8),
+                        lhsT=ident_bf16[:],
+                        rhs=raw_tiles[k][:, :, first_col + x : first_col + x + P].rearrange("p t (n i) -> p n t i", i=8),
+                        start=True,
+                        stop=True,
+                    )
+                banks_of[k].append(bank)
+
+        def copy_w_on_scalar(k):
+            if k >= W_PIECES:
+                return
+            if k in SCALAR_PIECES:
+                grouped_tiles[k, 0] = grouped_s_pool.tile([P, N_TILE, PACK], BF16, name="grouped_s", align_bytes=64)
+                nc.scalar.copy(
+                    out=grouped_tiles[k, 0][:].rearrange("p (n i) t -> p n t i", i=4),
+                    in_=raw_tiles[k][:, :, 0:N_TILE].rearrange("p t (n i) -> p n t i", i=4),
+                )
+            grouped = grouped_s_pool.tile([P, N_TILE, PACK], BF16, name="grouped_s", align_bytes=64)
+            for x, bank in enumerate(banks_of[k]):
+                nc.scalar.copy(out=grouped[:, x * PS_COLS : (x + 1) * PS_COLS, :], in_=bank[:])
             grouped_tiles[k, 1] = grouped
 
         def quantise_w(k, part):
@@ -298,8 +364,9 @@ def tile_multiscaleretention_pc_kernel(tc, ret, g, gn_weight, gn_bias, w_o, b_o,
         head_sums(1)
         shifts(0)
         for k in range(FIRST_PIECES):
+            regroup_w_on_tensor(k)
             regroup_w_on_vector(k)
-            regroup_w_on_scalar(k)
+            copy_w_on_scalar(k)
             load_w_piece(k + RAW_PIECES)
         load_tokens(g_rows, g_tiles, 1, "g_t")
         load_tokens(ret_rows, ret_tiles, 3, "ret_t")
@@ -311,8 +378,10 @@ def tile_multiscaleretention_pc_kernel(tc, ret, g, gn_weight, gn_bias, w_o, b_o,
             in_=affine_ps[:, 0 : HALVES * P].bitcast(BF16).rearrange("p (u x) -> p u x", u=HALVES)[:, :, 0 : 2 * PASSES * PAIR],
         )
         normalise(0)
+        normalise_on_vector(0)
         for k in range(FIRST_PIECES):
-            quantise_w(k, 0)
+            if k not in SCALAR_PIECES:
+                quantise_w(k, 0)
 
         sums = []
         for n in range(ROUNDS + 1):
@@ -321,11 +390,17 @@ def tile_multiscaleretention_pc_kernel(tc, ret, g, gn_weight, gn_bias, w_o, b_o,
             normalise(n + 1)
             affine_and_silu(n)
             for k in (first, first + 1):
-                regroup_w_on_scalar(k)
+                regroup_w_on_tensor(k)
+                copy_w_on_scalar(k)
+            normalise_on_vector(n + 1)
             regroup_w_on_vector(first)
             quantise_w(first - 2, 1)
+            part_g(n + 1)
             gate_product(n - 1)
-            quantise_w(first, 0)
+            if first not in SCALAR_PIECES:
+                quantise_w(first, 0)
+            if first - 2 in SCALAR_PIECES:
+                quantise_w(first - 2, 0)
             if n == 0 or n % TILE_ROUNDS == 1:
                 i = (n + 1) // TILE_ROUNDS + 1
                 reciprocal_deviations(i)
@@ -338,7 +413,10 @@ def tile_multiscaleretention_pc_kernel(tc, ret, g, gn_weight, gn_bias, w_o, b_o,
                 quantise_gate(n - 1)
             regroup_w_on_vector(first + 1)
             quantise_w(first - 1, 1)
-            quantise_w(first + 1, 0)
+            if first + 1 not in SCALAR_PIECES:
+                quantise_w(first + 1, 0)
+            if first - 1 in SCALAR_PIECES:
+                quantise_w(first - 1, 0)
             load_w_piece(first + RAW_PIECES)
             load_w_piece(first + RAW_PIECES + 1)
             if n > 0:

from contextlib import ExitStack

import concourse.mybir as mybir
from concourse.masks import make_identity

F32 = mybir.dt.float32
BF16 = mybir.dt.bfloat16
U32 = mybir.dt.uint32
U8 = mybir.dt.uint8
FP8X4 = mybir.dt.float8_e4m3fn_x4
ACT = mybir.ActivationFunctionType
ALU = mybir.AluOpType

P = 128
PACK = 4
PAIR = 2
HALVES = PACK // PAIR
K_PASS = P * PACK
TOKENS = 1024
TOKEN_TILES = TOKENS // P
E = 2048
D = 256
HEAD_P = D // PACK
EPS = 1e-5
PASSES = E // K_PASS
HEADS = E // D
N_TILE = 512
ROUND_PASSES = 2
ROUND_K = ROUND_PASSES * K_PASS
ROUND_HEADS = ROUND_K // D
TILE_ROUNDS = PASSES // ROUND_PASSES
ROUNDS = TOKEN_TILES * TILE_ROUNDS
WORDS = ROUND_PASSES * P
W_COLS = 1024
W_PIECES = (E // W_COLS) * PASSES
FIRST_PIECES = 1
PIECES_PER_STEP = 2
RAW_PIECES = 4
UNIT_TILES = W_COLS // N_TILE
UNITS = TOKEN_TILES * (E // W_COLS)
MX_LAG = 3

PS_COLS = 256

SCALAR_PIECES = (0, 2)
LAST_ROUNDS = 3
VECTOR_HEADS = 2
FLOPS = 2 * TOKENS * E * E


def tile_multiscaleretention_pc_kernel(tc, ret, g, gn_weight, gn_bias, w_o, b_o, out):
    nc = tc.nc
    ret_rows = ret.flatten_outer_dims()
    g_rows = g.flatten_outer_dims()
    out_rows = out.flatten_outer_dims()
    w_view = w_o.rearrange("(c p t) n -> c p t n", p=P, t=PACK)

    with ExitStack() as ctx:
        consts = ctx.enter_context(tc.tile_pool(name="consts", bufs=1))
        keep = ctx.enter_context(tc.tile_pool(name="keep", bufs=1))
        token_pool = ctx.enter_context(tc.tile_pool(name="token_pool", bufs=TOKEN_TILES))
        norm_pool = ctx.enter_context(tc.tile_pool(name="norm_pool", bufs=3))
        small = ctx.enter_context(tc.tile_pool(name="small", bufs=3))
        kmajor = ctx.enter_context(tc.tile_pool(name="kmajor", bufs=2))
        parted_pool = ctx.enter_context(tc.tile_pool(name="parted_pool", bufs=2))
        w_raw_pool = ctx.enter_context(tc.tile_pool(name="w_raw_pool", bufs=RAW_PIECES))
        grouped_v_pool = ctx.enter_context(tc.tile_pool(name="grouped_v_pool", bufs=2))
        grouped_s_pool = ctx.enter_context(tc.tile_pool(name="grouped_s_pool", bufs=5))
        out_pool = ctx.enter_context(tc.tile_pool(name="out_pool", bufs=6))
        psum_norm = ctx.enter_context(tc.psum_pool(name="psum_norm", bufs=2))
        psum_g = ctx.enter_context(tc.psum_pool(name="psum_g", bufs=2))
        psum_acc = ctx.enter_context(tc.psum_pool(name="psum_acc", bufs=4))
        ctx.enter_context(tc.manual_schedule())

        w_codes = keep.tile([P, PASSES, E], U32, align_bytes=64)
        w_scales = keep.tile([P, PASSES, E], U8, align_bytes=64)
        gate_codes = keep.tile([P, ROUNDS, WORDS], U32, align_bytes=64)
        gate_scales = keep.tile([P, ROUNDS, WORDS], U8, align_bytes=64)

        ret_tiles = {}
        g_tiles = {}
        raw_tiles = {}
        grouped_tiles = {}
        banks_of = {}

        def load_tokens(rows_of, tiles, i, name):
            if i < TOKEN_TILES:
                tiles[i] = token_pool.tile([P, E], BF16, name=name)
                nc.sync.dma_start(out=tiles[i][:], in_=rows_of[i * P : (i + 1) * P, :])

        def load_w_piece(k):
            if k < W_PIECES:
                jj, c = divmod(k, PASSES)
                raw_tiles[k] = w_raw_pool.tile([P, PACK, W_COLS], BF16, name="raw")
                for u in range(HALVES):
                    nc.sync.dma_start(
                        out=raw_tiles[k][:, u * PAIR : (u + 1) * PAIR, :],
                        in_=w_view[c, :, u * PAIR : (u + 1) * PAIR, jj * W_COLS : (jj + 1) * W_COLS],
                    )

        affine_rows = consts.tile([P, K_PASS], BF16)
        nc.gpsimd.memset(affine_rows[:], 0.0)
        load_tokens(ret_rows, ret_tiles, 0, "ret_t")
        load_w_piece(0)
        load_tokens(ret_rows, ret_tiles, 1, "ret_t")
        load_tokens(g_rows, g_tiles, 0, "g_t")
        nc.sync.dma_start(out=affine_rows[0:PASSES, :], in_=gn_weight.rearrange("(c x) -> c x", x=K_PASS))
        nc.sync.dma_start(out=affine_rows[PASSES : 2 * PASSES, :], in_=gn_bias.rearrange("(c x) -> c x", x=K_PASS))
        load_w_piece(1)
        load_tokens(ret_rows, ret_tiles, 2, "ret_t")
        load_w_piece(2)
        load_w_piece(3)

        neg_half = consts.tile([P, HEADS], F32)
        nc.gpsimd.memset(neg_half[:], -0.5)
        first_silu = consts.tile([P, 1], F32)
        nc.scalar.activation(out=first_silu[:], in_=neg_half[:, 0:1], func=ACT.Silu)
        ident_f32 = consts.tile([P, P], F32)
        make_identity(nc, ident_f32[:])
        ident_bf16 = consts.tile([P, P], BF16)
        make_identity(nc, ident_bf16[:])
        bias_all = consts.tile([P, E], BF16)
        affine_cols = consts.tile([P, HALVES, 2 * PASSES * PAIR], F32)

        stats_of = {}
        rstd_of = {}
        shift_of = {}
        norm_of = {}
        norm_T_of = {}
        g_T_of = {}
        parted_of = {}
        rn_T_of = {}
        silu_T_of = {}
        gate_grouped_of = {}

        def head_sums(i):
            if i >= TOKEN_TILES:
                return
            stats_of[i] = small.tile([P, HEADS, 3], F32, name="stats")
            for h in range(0, HEADS, 2):
                nc.vector.bn_stats(
                    out=stats_of[i][:, h : h + 2, :].rearrange("p h s -> p (h s)"),
                    in_=ret_tiles[i][:, h * D : (h + 2) * D].rearrange("p (h d) -> p d h", h=2),
                )

        def reciprocal_deviations(i):
            if i >= TOKEN_TILES:
                return
            var_eps = small.tile([P, HEADS], F32, name="var_eps")
            nc.vector.tensor_scalar(
                out=var_eps[:], in0=stats_of[i][:, :, 2], scalar1=1.0 / D, scalar2=EPS, op0=ALU.mult, op1=ALU.add
            )
            rstd_of[i] = small.tile([P, HEADS], F32, name="rstd")
            nc.gpsimd.tensor_tensor(out=rstd_of[i][:], in0=var_eps[:], in1=neg_half[:], op=ALU.pow)

        def shifts(i):
            if i >= TOKEN_TILES:
                return
            shift_of[i] = small.tile([P, HEADS], F32, name="shift")
            nc.vector.scalar_tensor_tensor(
                out=shift_of[i][:], in0=stats_of[i][:, :, 1], scalar=-1.0, in1=rstd_of[i][:], op0=ALU.mult, op1=ALU.mult
            )

        def vector_heads(n):
            return VECTOR_HEADS if n >= ROUNDS - LAST_ROUNDS else 0

        def normalise(n):
            if n >= ROUNDS:
                return
            i, half = divmod(n, TILE_ROUNDS)
            norm = norm_pool.tile([P, ROUND_PASSES, PACK, P], F32, name="norm")
            norm_of[n] = norm
            for h in range(vector_heads(n), ROUND_HEADS):
                first_col = half * ROUND_K + h * D
                cr, hh = divmod(h, 2)
                nc.scalar.activation(
                    out=norm[:, cr, :, hh * HEAD_P : (hh + 1) * HEAD_P],
                    in_=ret_tiles[i][:, first_col : first_col + D].rearrange("p (q t) -> p t q", t=PACK),
                    func=ACT.Identity,
                    scale=rstd_of[i][:, half * ROUND_HEADS + h : half * ROUND_HEADS + h + 1],
                    bias=shift_of[i][:, half * ROUND_HEADS + h : half * ROUND_HEADS + h + 1],
                )

        def normalise_on_vector(n):
            if n >= ROUNDS:
                return
            i, half = divmod(n, TILE_ROUNDS)
            for h in range(vector_heads(n)):
                first_col = half * ROUND_K + h * D
                cr, hh = divmod(h, 2)
                nc.vector.tensor_scalar(
                    out=norm_of[n][:, cr, :, hh * HEAD_P : (hh + 1) * HEAD_P],
                    in0=ret_tiles[i][:, first_col : first_col + D].rearrange("p (q t) -> p t q", t=PACK),
                    scalar1=rstd_of[i][:, half * ROUND_HEADS + h : half * ROUND_HEADS + h + 1],
                    scalar2=shift_of[i][:, half * ROUND_HEADS + h : half * ROUND_HEADS + h + 1],
                    op0=ALU.mult,
                    op1=ALU.add,
                )

        def part_g(n):
            if n >= ROUNDS or not (n >= ROUNDS - LAST_ROUNDS):
                return
            i, half = divmod(n, TILE_ROUNDS)
            parted_of[n] = parted_pool.tile([P, ROUND_PASSES, HALVES, P], F32, name="parted")
            nc.vector.tensor_copy(out=parted_of[n][:], in_=g_tiles[i][:].bitcast(F32)[:, half * ROUND_K // 2 : (half + 1) * ROUND_K // 2].rearrange("p (c q u) -> p c u q", c=ROUND_PASSES, u=HALVES))

        def transposes(n):
            if n >= ROUNDS:
                return
            i, half = divmod(n, TILE_ROUNDS)
            norm_T = [psum_norm.tile([P, PACK, P], F32, name="norm_T%d" % cr, tag="norm_T") for cr in range(ROUND_PASSES)]
            for cr in range(ROUND_PASSES):
                for t in range(PACK):
                    nc.tensor.transpose(norm_T[cr][:, t, :], norm_of[n][:, cr, t, :], ident_f32[:])
            g_T = psum_g.tile([P, HALVES * WORDS], F32, name="g_T")
            g_words = g_tiles[i][:].bitcast(F32)
            if n in parted_of:
                for u in range(HALVES):
                    for cr in range(ROUND_PASSES):
                        nc.tensor.transpose(g_T[:, u * WORDS + cr * P : u * WORDS + (cr + 1) * P], parted_of[n][:, cr, u, :], ident_f32[:])
                norm_T_of[n] = norm_T
                g_T_of[n] = g_T
                return
            for u in range(HALVES):
                for cr in range(ROUND_PASSES):
                    first_word = (half * ROUND_K + cr * K_PASS) // PAIR
                    nc.tensor.transpose(
                        g_T[:, u * WORDS + cr * P : u * WORDS + (cr + 1) * P],
                        g_words[:, first_word + u : first_word + K_PASS // PAIR : HALVES],
                        ident_f32[:],
                    )
            norm_T_of[n] = norm_T
            g_T_of[n] = g_T

        def affine_and_silu(n):
            if n >= ROUNDS:
                return
            half = n % TILE_ROUNDS
            rn_T = kmajor.tile([P, PACK, WORDS], F32, name="rn_T")
            for cr in range(ROUND_PASSES):
                for t in range(PACK):
                    u, e = divmod(t, PAIR)
                    w_col = (half * ROUND_PASSES + cr) * PAIR + e
                    b_col = PASSES * PAIR + w_col
                    nc.scalar.activation(
                        out=rn_T[:, t, cr * P : (cr + 1) * P], in_=norm_T_of[n][cr][:, t, :], func=ACT.Identity,
                        scale=affine_cols[:, u, w_col : w_col + 1], bias=affine_cols[:, u, b_col : b_col + 1],
                    )
            silu_T = kmajor.tile([P, PACK, WORDS], F32, name="silu_T")
            nc.scalar.activation(
                out=silu_T[:].rearrange("p (u e) x -> p u e x", e=PAIR),
                in_=g_T_of[n][:].bitcast(BF16).rearrange("p (u x e) -> p u e x", u=HALVES, e=PAIR),
                func=ACT.Silu,
            )
            rn_T_of[n] = rn_T
            silu_T_of[n] = silu_T

        def gate_product(n):
            if n < 0 or n >= ROUNDS:
                return
            gate_grouped = kmajor.tile([P, WORDS, PACK], BF16, name="gate_grouped", align_bytes=64)
            nc.vector.tensor_tensor(
                out=gate_grouped[:].rearrange("p (n i) t -> p n t i", i=4),
                in0=rn_T_of[n][:].rearrange("p t (n i) -> p n t i", i=4),
                in1=silu_T_of[n][:].rearrange("p t (n i) -> p n t i", i=4),
                op=ALU.mult,
            )
            gate_grouped_of[n] = gate_grouped

        def quantise_gate(n):
            if n < 0 or n >= ROUNDS:
                return
            nc.vector.quantize_mx(
                out=gate_codes[:, n, :].bitcast(FP8X4),
                scales=gate_scales[:, n, :],
                in_=gate_grouped_of[n][:].rearrange("p x t -> p (x t)"),
            )

        def regroup_w_on_vector(k):
            if k >= W_PIECES:
                return
            if k in SCALAR_PIECES:
                return
            grouped = grouped_v_pool.tile([P, N_TILE, PACK], BF16, name="grouped_v", align_bytes=64)
            nc.vector.tensor_copy(
                out=grouped[:].rearrange("p (n i) t -> p n t i", i=4),
                in_=raw_tiles[k][:, :, 0:N_TILE].rearrange("p t (n i) -> p n t i", i=4),
            )
            grouped_tiles[k, 0] = grouped

        def regroup_w_on_tensor(k):
            if k >= W_PIECES:
                return
            banks_of[k] = []
            for first_col in range(N_TILE, W_COLS, PS_COLS):
                bank = psum_acc.tile([P, PS_COLS, PACK], BF16, name="bank", tag="acc")
                for x in range(0, PS_COLS, P):
                    nc.tensor.matmul(
                        out=bank[:, x : x + P, :].rearrange("p (n i) t -> p n t i", i=8),
                        lhsT=ident_bf16[:],
                        rhs=raw_tiles[k][:, :, first_col + x : first_col + x + P].rearrange("p t (n i) -> p n t i", i=8),
                        start=True,
                        stop=True,
                    )
                banks_of[k].append(bank)

        def copy_w_on_scalar(k):
            if k >= W_PIECES:
                return
            if k in SCALAR_PIECES:
                grouped_tiles[k, 0] = grouped_s_pool.tile([P, N_TILE, PACK], BF16, name="grouped_s", align_bytes=64)
                nc.scalar.copy(
                    out=grouped_tiles[k, 0][:].rearrange("p (n i) t -> p n t i", i=4),
                    in_=raw_tiles[k][:, :, 0:N_TILE].rearrange("p t (n i) -> p n t i", i=4),
                )
            grouped = grouped_s_pool.tile([P, N_TILE, PACK], BF16, name="grouped_s", align_bytes=64)
            for x, bank in enumerate(banks_of[k]):
                nc.scalar.copy(out=grouped[:, x * PS_COLS : (x + 1) * PS_COLS, :], in_=bank[:])
            grouped_tiles[k, 1] = grouped

        def quantise_w(k, part):
            if k < 0 or k >= W_PIECES:
                return
            jj, c = divmod(k, PASSES)
            n_cols = slice(jj * W_COLS + part * N_TILE, jj * W_COLS + (part + 1) * N_TILE)
            nc.vector.quantize_mx(
                out=w_codes[:, c, n_cols].bitcast(FP8X4),
                scales=w_scales[:, c, n_cols],
                in_=grouped_tiles[k, part][:].rearrange("p n t -> p (n t)"),
            )

        def open_sums(i, columns, pool=None, tag="acc"):
            sums = []
            for j in columns:
                acc = (pool or psum_acc).tile([P, N_TILE], F32, name="acc", tag=tag)
                sums.append((acc, i, j))
            return sums

        def multiply(sums, passes):
            for acc, i, j in sums:
                n_cols = slice(j * N_TILE, (j + 1) * N_TILE)
                for c in passes:
                    half, cr = divmod(c, ROUND_PASSES)
                    made_in = i * TILE_ROUNDS + half
                    nc.tensor.matmul_mx(
                        out=acc[:],
                        lhsT=gate_codes[:, made_in, cr * P : (cr + 1) * P].bitcast(FP8X4),
                        lhsT_scale=gate_scales[:, made_in, cr * P : (cr + 1) * P],
                        rhs=w_codes[:, c, n_cols].bitcast(FP8X4),
                        rhs_scale=w_scales[:, c, n_cols],
                        start=(c == 0),
                        stop=(c == PASSES - 1),
                    )

        def add_bias_and_store(sums):
            for acc, i, j in sums:
                n_cols = slice(j * N_TILE, (j + 1) * N_TILE)
                result = out_pool.tile([P, N_TILE], F32, name="result")
                nc.vector.tensor_tensor(out=result[:], in0=acc[:], in1=bias_all[:, n_cols], op=ALU.add)
                nc.sync.dma_start(out=out_rows[i * P : (i + 1) * P, n_cols], in_=result[:])

        head_sums(0)
        reciprocal_deviations(0)
        head_sums(1)
        shifts(0)
        for k in range(FIRST_PIECES):
            regroup_w_on_tensor(k)
            regroup_w_on_vector(k)
            copy_w_on_scalar(k)
            load_w_piece(k + RAW_PIECES)
        load_tokens(g_rows, g_tiles, 1, "g_t")
        load_tokens(ret_rows, ret_tiles, 3, "ret_t")
        affine_ps = psum_g.tile([P, HALVES * WORDS], F32, tag="g_T")
        for u in range(HALVES):
            nc.tensor.transpose(affine_ps[:, u * P : (u + 1) * P], affine_rows[:].bitcast(F32)[:, u::HALVES], ident_f32[:])
        nc.vector.tensor_copy(
            out=affine_cols[:],
            in_=affine_ps[:, 0 : HALVES * P].bitcast(BF16).rearrange("p (u x) -> p u x", u=HALVES)[:, :, 0 : 2 * PASSES * PAIR],
        )
        normalise(0)
        normalise_on_vector(0)
        for k in range(FIRST_PIECES):
            if k not in SCALAR_PIECES:
                quantise_w(k, 0)

        sums = []
        for n in range(ROUNDS + 1):
            first = FIRST_PIECES + n * PIECES_PER_STEP
            transposes(n)
            normalise(n + 1)
            affine_and_silu(n)
            for k in (first, first + 1):
                regroup_w_on_tensor(k)
                copy_w_on_scalar(k)
            normalise_on_vector(n + 1)
            regroup_w_on_vector(first)
            quantise_w(first - 2, 1)
            part_g(n + 1)
            gate_product(n - 1)
            if first not in SCALAR_PIECES:
                quantise_w(first, 0)
            if first - 2 in SCALAR_PIECES:
                quantise_w(first - 2, 0)
            if n == 0 or n % TILE_ROUNDS == 1:
                i = (n + 1) // TILE_ROUNDS + 1
                reciprocal_deviations(i)
                add_bias_and_store(sums)
                head_sums(i + 1)
                shifts(i)
                quantise_gate(n - 1)
            else:
                add_bias_and_store(sums)
                quantise_gate(n - 1)
            regroup_w_on_vector(first + 1)
            quantise_w(first - 1, 1)
            if first + 1 not in SCALAR_PIECES:
                quantise_w(first + 1, 0)
            if first - 1 in SCALAR_PIECES:
                quantise_w(first - 1, 0)
            load_w_piece(first + RAW_PIECES)
            load_w_piece(first + RAW_PIECES + 1)
            if n > 0:
                load_tokens(g_rows, g_tiles, n + 1, "g_t")
                if n > 1:
                    load_tokens(ret_rows, ret_tiles, n + 2, "ret_t")
            if n == 1:
                nc.sync.dma_start(out=bias_all[:], in_=b_o.partition_broadcast(P))
            sums = []
            for i in range(TOKEN_TILES - 1):
                for j in range(E // N_TILE):
                    if n == TILE_ROUNDS * i + MX_LAG + j // 2:
                        block = open_sums(i, [j])
                        multiply(block, range(PASSES))
                        sums += block
            if n == ROUNDS:
                last = open_sums(TOKEN_TILES - 1, (0, 1), psum_norm, "norm_T")
                last += open_sums(TOKEN_TILES - 1, (2, 3))
                multiply(last, range(ROUND_PASSES))
                multiply(last, range(ROUND_PASSES, PASSES))
                sums += last
        add_bias_and_store(sums)
